import numpy as np
import ml_dtypes


def mxq(x, axis, fmt="e4m3"):
    dtype, down = {"e4m3": (ml_dtypes.float8_e4m3fn, 7), "e5m2": (ml_dtypes.float8_e5m2, 14)}[fmt]
    v = np.moveaxis(np.asarray(x, np.float32).astype(ml_dtypes.bfloat16).astype(np.float64), axis, -1)
    blocks = v.reshape(v.shape[:-1] + (-1, 32))
    amax = np.abs(blocks).max(-1, keepdims=True)
    byte = np.maximum(np.where(amax > 0, np.frexp(amax)[1] - 1 + 127, 0) - down, 1)
    scale = np.exp2(byte - 127.0)
    codes = (blocks / scale).astype(np.float32).astype(dtype).astype(np.float64)
    return np.moveaxis((codes * scale).reshape(v.shape), -1, axis)


WIDE = False


def mx_kscale(k):
    if not WIDE:
        return np.ones(k)
    levels = np.array([10, -10, 5, -5, 0])
    a = np.random.permutation(np.resize(levels, k // 512 * 4)).reshape(k // 512, 4)
    idx = np.arange(k)
    return np.exp2(a[idx // 512, idx % 128 // 32])


BF16 = ml_dtypes.bfloat16


def bf(x):
    return np.asarray(x, np.float32).astype(BF16)


def f64(x):
    return np.asarray(x).astype(np.float64)


E2M1 = np.array([0.0, 0.5, 1.0, 1.5, 2.0, 3.0, 4.0, 6.0, -0.0, -0.5, -1.0, -1.5, -2.0, -3.0, -4.0, -6.0])


def pack_weight(w, fmt):
    k, n = w.shape
    w = f64(bf(w)).reshape(k // 32, 32, n)
    amax = np.abs(w).max(1)
    if fmt == "e4m3":
        byte = np.frexp(amax)[1] - 1 + 127 - 7
    else:
        mant, ex = np.frexp(amax / 6.0)
        byte = np.where(mant > 0.5, ex, ex - 1) + 127
    byte = np.clip(np.where(amax > 0, byte, 1), 1, 254)
    scaled = (w * np.exp2(127.0 - byte)[:, None, :]).reshape(k, n).astype(np.float32)
    by_word = np.ascontiguousarray(scaled.reshape(k // 512, 128, 4, n).transpose(0, 1, 3, 2))
    if fmt == "e4m3":
        words = by_word.astype(ml_dtypes.float8_e4m3fn).view(np.uint8)
    else:
        c = by_word.astype(ml_dtypes.float4_e2m1fn).view(np.uint8) & 0xF
        words = c[..., 0::2] | (c[..., 1::2] << 4)
    return np.ascontiguousarray(words), np.ascontiguousarray(byte.astype(np.uint8).reshape(k // 512, 16, n))


def unpack_weight(words, scales, fmt):
    g, p, n, _ = words.shape
    if fmt == "e4m3":
        vals = np.ascontiguousarray(words).view(ml_dtypes.float8_e4m3fn).astype(np.float64)
    else:
        nib = np.empty((g, p, n, 4), np.uint8)
        nib[..., 0::2] = words & 0xF
        nib[..., 1::2] = words >> 4
        vals = E2M1[nib]
    vals = vals * np.repeat(np.exp2(scales.astype(np.float64) - 127.0), 8, axis=1)[..., None]
    return vals.transpose(0, 1, 3, 2).reshape(g * 512, n)


B, C, H, L = 1, 2048, 2048, 128


def sigmoid(v):
    return 1.0 / (1.0 + np.exp(-v))


def pconv(xq, W_words, W_scales, b):
    return (unpack_weight(W_words, W_scales, "e4m3").T @ xq) + f64(b)[None, :, None]


def setup_inputs():
    s = np.concatenate([mx_kscale(C + H)[:C], np.ones(H)])
    w = lambda: pack_weight(np.ascontiguousarray((np.random.standard_normal((H, C + H)) / np.sqrt(C + H) / s).T), "e4m3")
    b = lambda: bf(np.random.standard_normal(H) * 0.3)
    inp = bf(np.random.standard_normal((B, C, L)) * s[:C, None])
    h = bf(np.random.standard_normal((B, H, L)))
    W_r_words, W_r_scales = w()
    b_r = b()
    W_u_words, W_u_scales = w()
    b_u = b()
    W_h_words, W_h_scales = w()
    b_h = b()
    return {"input": inp, "h": h,
            "W_r_words": W_r_words, "W_r_scales": W_r_scales, "b_r": b_r,
            "W_u_words": W_u_words, "W_u_scales": W_u_scales, "b_u": b_u,
            "W_h_words": W_h_words, "W_h_scales": W_h_scales, "b_h": b_h}


def reference(input, h, W_r_words, W_r_scales, b_r, W_u_words, W_u_scales, b_u, W_h_words, W_h_scales, b_h):
    h = f64(h)
    xq = mxq(f64(input), 1, "e4m3")
    input_h = np.concatenate([xq, mxq(h, 1, "e4m3")], axis=1)
    reset_h = sigmoid(pconv(input_h, W_r_words, W_r_scales, b_r))
    update_h = sigmoid(pconv(input_h, W_u_words, W_u_scales, b_u))
    input_new_h = np.concatenate([xq, mxq(h * reset_h, 1, "e4m3")], axis=1)
    new_h = np.tanh(pconv(input_new_h, W_h_words, W_h_scales, b_h))
    return (1.0 - update_h) * new_h + update_h * h

@@ -1,0 +1,240 @@
+from contextlib import ExitStack
+
+import concourse.mybir as mybir
+from concourse.masks import make_identity
+
+FP8X4 = mybir.dt.float8_e4m3fn_x4
+BF16 = mybir.dt.bfloat16
+F32 = mybir.dt.float32
+I32 = mybir.dt.int32
+U8 = mybir.dt.uint8
+ACT = mybir.ActivationFunctionType
+ALU = mybir.AluOpType
+
+P = 128
+L = 128
+CH = 2048
+NG = 8
+FLOPS = 3 * 2 * 4096 * 2048 * 128
+
+PIN = False
+W_BUFS = 17
+H_RECTS = (
+    (0, 2, 0, 1024), (2, 4, 0, 1024), (4, 6, 0, 1024), (6, 8, 0, 1024),
+    (0, 2, 1024, 2048), (2, 4, 1024, 2048),
+    (4, 8, 1024, 1536),
+    (4, 6, 1536, 2048), (6, 8, 1536, 2048),
+)
+
+
+def tile_gru_w_kernel(tc, inp, h, W_r_words, W_r_scales, b_r, W_u_words, W_u_scales, b_u,
+                                 W_h_words, W_h_scales, b_h, out):
+    nc = tc.nc
+    words = (W_r_words, W_u_words, W_h_words)
+    scales = (W_r_scales, W_u_scales, W_h_scales)
+    biases = (b_r, b_u, b_h)
+    out_v = out[0].rearrange("(j m) l -> m j l", m=P)
+
+    with ExitStack() as ctx:
+        const = ctx.enter_context(tc.tile_pool(name="const", bufs=1))
+        wpool = ctx.enter_context(tc.tile_pool(name="wpool", bufs=W_BUFS))
+        work = ctx.enter_context(tc.tile_pool(name="work", bufs=4))
+        ps_lv = ctx.enter_context(tc.psum_pool(name="ps_lv", bufs=1))
+        ps_jb = ctx.enter_context(tc.psum_pool(name="ps_jb", bufs=2))
+        ps_tp = ctx.enter_context(tc.psum_pool(name="ps_tp", bufs=2))
+        if PIN:
+            ctx.enter_context(tc.manual_schedule())
+
+        planes = const.tile([P, 6, CH], U8, name="planes", align_bytes=64)
+        x_raw = const.tile([P, NG, 4, L], BF16, name="x_raw")
+        x_grp = const.tile([P, NG, L, 4], BF16, name="x_grp", align_bytes=64)
+        x_codes = const.tile([P, NG, L], I32, name="x_codes", align_bytes=64)
+        x_scales = const.tile([P, NG, L], U8, name="x_scales", align_bytes=64)
+        ident = const.tile([P, P], BF16, name="ident")
+        b_raw = const.tile([P, P], BF16, name="b_raw")
+        bias = const.tile([P, P], F32, name="bias")
+        hT = const.tile([P, CH], BF16, name="hT")
+        h_c = const.tile([P, 16, L], BF16, name="h_c")
+        hr_c = const.tile([P, 16, L], BF16, name="hr_c")
+        hrT = const.tile([P, CH], BF16, name="hrT")
+        hr_grp = const.tile([P, 4, L, 4], BF16, name="hr_grp", align_bytes=64)
+        hr_codes = const.tile([P, 4, L], I32, name="hr_codes", align_bytes=64)
+        hr_scales = const.tile([P, 4, L], U8, name="hr_scales", align_bytes=64)
+        one_minus_u = const.tile([P, 16, L], F32, name="one_minus_u")
+        blend = const.tile([P, 16, L], F32, name="blend")
+
+        wmap = {}
+
+        def load_scales(gate):
+            src = scales[gate].bitcast(I32)
+            for hf in range(2):
+                for quad in (0, 2, 1, 3):
+                    nc.sync.dma_start(
+                        out=planes[32 * quad:32 * quad + 16, 2 * gate + hf, :].bitcast(I32),
+                        in_=src[4 * hf:4 * hf + 4, 4 * quad:4 * quad + 4, :],
+                    )
+
+        def load_rect(gate, g0, g1, c0, c1):
+            ng = g1 - g0
+            ncol = c1 - c0
+            wt = wpool.tile([P, CH], I32, name="wt", tag="w", align_bytes=64)
+            view = wt[:, 0:ng * ncol].rearrange("p (g n) -> p g n", g=ng)
+            src = words[gate].rearrange("g p n t -> p g (n t)")[:, g0:g1, 4 * c0:4 * c1].bitcast(I32)
+            nc.sync.dma_start(out=view, in_=src)
+            for g in range(g0, g1):
+                for j in range(c0 // P, c1 // P):
+                    wmap[(gate, g, j)] = view[:, g - g0, P * j - c0:P * j - c0 + P]
+
+        def mx(ps_ap, gate, g, j):
+            if gate == 2 and g >= 4:
+                rhs = hr_codes[:, g - 4, :]
+                rhs_scale = hr_scales[:, g - 4, :]
+            else:
+                rhs = x_codes[:, g, :]
+                rhs_scale = x_scales[:, g, :]
+            nc.tensor.matmul_mx(
+                out=ps_ap,
+                lhsT=wmap[(gate, g, j)].bitcast(FP8X4),
+                lhsT_scale=planes[4 * (g % 4):P, 2 * gate + g // 4, P * j:P * j + P],
+                rhs=rhs.bitcast(FP8X4),
+                rhs_scale=rhs_scale,
+                start=(g == 0),
+                stop=(g == NG - 1),
+            )
+
+        def post(gate, q, ps_list, fine=False):
+            act = work.tile([P, 4, L], F32, name="act", tag="act")
+            func = ACT.Tanh if gate == 2 else ACT.Sigmoid
+            pieces = [(a, a + 1) for a in range(4)] if fine else [(0, 4)]
+            for a in range(4):
+                col = 16 * gate + 4 * q + a
+                nc.scalar.activation(out=act[:, a, :], in_=ps_list[a], func=func,
+                                     bias=bias[:, col:col + 1], scale=1.0)
+            for lo, hi in pieces:
+                pc = slice(lo, hi)
+                sl = slice(4 * q + lo, 4 * q + hi)
+                if gate == 0:
+                    nc.vector.tensor_tensor(out=hr_c[:, sl, :], in0=act[:, pc, :], in1=h_c[:, sl, :], op=ALU.mult)
+                elif gate == 1:
+                    nc.vector.tensor_scalar(out=one_minus_u[:, sl, :], in0=act[:, pc, :], scalar1=-1.0,
+                                            scalar2=1.0, op0=ALU.mult, op1=ALU.add)
+                    nc.vector.tensor_tensor(out=blend[:, sl, :], in0=act[:, pc, :], in1=h_c[:, sl, :], op=ALU.mult)
+                else:
+                    nc.vector.tensor_tensor(out=act[:, pc, :], in0=act[:, pc, :], in1=one_minus_u[:, sl, :],
+                                            op=ALU.mult)
+                    nc.vector.tensor_tensor(out=blend[:, sl, :], in0=act[:, pc, :], in1=blend[:, sl, :],
+                                            op=ALU.add)
+                    nc.sync.dma_start(out=out_v[:, sl, :], in_=blend[:, sl, :])
+
+        def live_tiles():
+            return [ps_lv.tile([P, L], F32, name="lv%d" % a, tag="lv%d" % a) for a in range(4)]
+
+        def quad_major(gate, q):
+            jb = ps_jb.tile([P, 4, L], F32, name="jb", tag="jb")
+            for a in range(4):
+                for g in range(NG):
+                    mx(jb[:, a, :], gate, g, 4 * q + a)
+            post(gate, q, [jb[:, a, :] for a in range(4)])
+
+        def gate_by_g(gate):
+            lv = live_tiles()
+            for g in range(NG):
+                for a in range(4):
+                    mx(lv[a][:], gate, g, a)
+            post(gate, 0, [t[:] for t in lv])
+            for q in range(1, 4):
+                quad_major(gate, q)
+
+        for gate in range(3):
+            nc.vector.memset(planes[:, 2 * gate:2 * gate + 2, :].bitcast(I32), 0)
+        nc.vector.memset(b_raw[:], 0.0)
+        make_identity(nc, ident[:])
+
+        nc.sync.dma_start(out=x_raw[:, 4:8, :, :].rearrange("p g t l -> p g (t l)"),
+                          in_=h[0].rearrange("(g p t) l -> p g (t l)", g=4, p=P, t=4))
+        nc.sync.dma_start(out=x_raw[:, 0:4, :, :].rearrange("p g t l -> p g (t l)"),
+                          in_=inp[0].rearrange("(g p t) l -> p g (t l)", g=4, p=P, t=4))
+        for gate in range(3):
+            nc.scalar.dma_start(out=b_raw[16 * gate:16 * gate + 16, :],
+                                in_=biases[gate].rearrange("(j m) -> j m", m=P))
+        for gate in range(2):
+            load_scales(gate)
+            for g in range(NG):
+                load_rect(gate, g, g + 1, 0, CH)
+
+        for half in (1, 0):
+            gs = slice(4 * half, 4 * half + 4)
+            nc.vector.tensor_copy(out=x_grp[:, gs, :, :], in_=x_raw[:, gs, :, :].rearrange("p g t l -> p g l t"))
+        for half in (1, 0):
+            gs = slice(4 * half, 4 * half + 4)
+            nc.vector.quantize_mx(
+                out=x_codes[:, gs, :].rearrange("p g l -> p (g l)").bitcast(FP8X4),
+                scales=x_scales[:, gs, :].rearrange("p g l -> p (g l)"),
+                in_=x_grp[:, gs, :, :].rearrange("p g l t -> p (g l t)"),
+            )
+
+        pb = ps_tp.tile([P, P], BF16, name="pb", tag="tp")
+        nc.tensor.transpose(pb[:], b_raw[:], ident[:])
+        nc.vector.tensor_copy(out=bias[:], in_=pb[:])
+
+        for b in range(2):
+            pt = ps_tp.tile([P, 8, P], BF16, name="pt", tag="tp")
+            for g2 in range(2):
+                for t in range(4):
+                    nc.tensor.transpose(pt[:, 4 * g2 + t, :], x_raw[:, 4 + 2 * b + g2, t, :], ident[:])
+            dst = hT[:, 1024 * b:1024 * b + 1024].rearrange("l (g p t) -> l g p t", g=2, t=4)
+            src = pt[:].rearrange("l (g t) p -> l g p t", g=2)
+            if b == 0:
+                nc.vector.tensor_copy(out=dst, in_=src)
+            else:
+                nc.scalar.copy(out=dst, in_=src)
+        for b in range(2):
+            pc = ps_tp.tile([P, 8, L], BF16, name="pc", tag="tp")
+            for jj in range(8):
+                nc.tensor.transpose(pc[:, jj, :], hT[:, 1024 * b + P * jj:1024 * b + P * jj + P], ident[:])
+            if b == 0:
+                nc.vector.tensor_copy(out=h_c[:, 0:8, :], in_=pc[:])
+            else:
+                nc.scalar.copy(out=h_c[:, 8:16, :], in_=pc[:])
+
+        gate_by_g(0)
+
+        load_scales(2)
+        for rect in H_RECTS:
+            load_rect(2, rect[0], rect[1], rect[2], rect[3])
+
+        for b in range(2):
+            pt = ps_tp.tile([P, 8, P], BF16, name="pt2", tag="tp")
+            for jj in range(8):
+                nc.tensor.transpose(pt[:, jj, :], hr_c[:, 8 * b + jj, :], ident[:])
+            dst = hrT[:, 1024 * b:1024 * b + 1024].rearrange("l (g t p) -> l g t p", g=2, t=4)
+            src = pt[:].rearrange("l j m -> l (j m)").rearrange("l (g p t) -> l g t p", g=2, t=4)
+            nc.vector.tensor_copy(out=dst, in_=src)
+            pq = ps_tp.tile([P, 8, L], BF16, name="pq", tag="tp")
+            for k in range(8):
+                nc.tensor.transpose(pq[:, k, :], hrT[:, 1024 * b + P * k:1024 * b + P * k + P], ident[:])
+            gs = slice(2 * b, 2 * b + 2)
+            nc.scalar.copy(out=hr_grp[:, gs, :, :], in_=pq[:].rearrange("p (g t) l -> p g l t", g=2))
+            nc.vector.quantize_mx(
+                out=hr_codes[:, gs, :].rearrange("p g l -> p (g l)").bitcast(FP8X4),
+                scales=hr_scales[:, gs, :].rearrange("p g l -> p (g l)"),
+                in_=hr_grp[:, gs, :, :].rearrange("p g l t -> p (g l t)"),
+            )
+
+        gate_by_g(1)
+
+        lv = live_tiles()
+        for g in range(NG):
+            for a in range(4):
+                mx(lv[a][:], 2, g, a)
+        post(2, 0, [t[:] for t in lv])
+        quad_major(2, 1)
+        lv = live_tiles()
+        for g in range(4):
+            for a in range(4):
+                mx(lv[a][:], 2, g, 12 + a)
+        quad_major(2, 2)
+        for g in range(4, NG):
+            for a in range(4):
+                mx(lv[a][:], 2, g, 12 + a)
+        post(2, 3, [t[:] for t in lv], fine=True)

@@ -74,6 +74,15 @@ def tile_gru_w_kernel(tc, inp, h, W_r_words, W_r_scales, b_r, W_u_words, W_u_sca
                         in_=src[4 * hf:4 * hf + 4, 4 * quad:4 * quad + 4, :],
                     )
 
+        def load_scales_sw(gate):
+            src = scales[gate].bitcast(F32).rearrange("(hf a) q n -> a hf q n", hf=2)
+            for quad in (0, 2, 1, 3):
+                for r in range(4):
+                    nc.gpsimd.dma_start(
+                        out=planes[32 * quad + r:32 * quad + 16:4, 2 * gate:2 * gate + 2, :].bitcast(F32),
+                        in_=src[:, :, 4 * quad + r, :],
+                    )
+
         def load_rect(gate, g0, g1, c0, c1):
             ng = g1 - g0
             ncol = c1 - c0
@@ -157,8 +166,10 @@ def tile_gru_w_kernel(tc, inp, h, W_r_words, W_r_scales, b_r, W_u_words, W_u_sca
         for gate in range(3):
             nc.scalar.dma_start(out=b_raw[16 * gate:16 * gate + 16, :],
                                 in_=biases[gate].rearrange("(j m) -> j m", m=P))
+        load_scales_sw(1)
+        load_scales_sw(2)
+        load_scales(0)
         for gate in range(2):
-            load_scales(gate)
             for g in range(NG):
                 load_rect(gate, g, g + 1, 0, CH)
 
@@ -199,7 +210,6 @@ def tile_gru_w_kernel(tc, inp, h, W_r_words, W_r_scales, b_r, W_u_words, W_u_sca
 
         gate_by_g(0)
 
-        load_scales(2)
         for rect in H_RECTS:
             load_rect(2, rect[0], rect[1], rect[2], rect[3])
 

@@ -17,14 +17,9 @@ CH = 2048
 NG = 8
 FLOPS = 3 * 2 * 4096 * 2048 * 128
 
-PIN = False
-W_BUFS = 17
-H_RECTS = (
-    (0, 2, 0, 1024), (2, 4, 0, 1024), (4, 6, 0, 1024), (6, 8, 0, 1024),
-    (0, 2, 1024, 2048), (2, 4, 1024, 2048),
-    (4, 8, 1024, 1536),
-    (4, 6, 1536, 2048), (6, 8, 1536, 2048),
-)
+PIN = True
+W_BUFS = 16
+SW_SCALES = (False, True, True)
 
 
 def tile_gru_w_kernel(tc, inp, h, W_r_words, W_r_scales, b_r, W_u_words, W_u_scales, b_u,
@@ -39,9 +34,7 @@ def tile_gru_w_kernel(tc, inp, h, W_r_words, W_r_scales, b_r, W_u_words, W_u_sca
         const = ctx.enter_context(tc.tile_pool(name="const", bufs=1))
         wpool = ctx.enter_context(tc.tile_pool(name="wpool", bufs=W_BUFS))
         work = ctx.enter_context(tc.tile_pool(name="work", bufs=4))
-        ps_lv = ctx.enter_context(tc.psum_pool(name="ps_lv", bufs=1))
-        ps_jb = ctx.enter_context(tc.psum_pool(name="ps_jb", bufs=2))
-        ps_tp = ctx.enter_context(tc.psum_pool(name="ps_tp", bufs=2))
+        psum = ctx.enter_context(tc.psum_pool(name="psum", bufs=1))
         if PIN:
             ctx.enter_context(tc.manual_schedule())
 
@@ -66,22 +59,22 @@ def tile_gru_w_kernel(tc, inp, h, W_r_words, W_r_scales, b_r, W_u_words, W_u_sca
         wmap = {}
 
         def load_scales(gate):
-            src = scales[gate].bitcast(I32)
-            for hf in range(2):
+            if SW_SCALES[gate]:
+                src = scales[gate].bitcast(F32).rearrange("(hf a) q n -> a hf q n", hf=2)
                 for quad in (0, 2, 1, 3):
-                    nc.sync.dma_start(
-                        out=planes[32 * quad:32 * quad + 16, 2 * gate + hf, :].bitcast(I32),
-                        in_=src[4 * hf:4 * hf + 4, 4 * quad:4 * quad + 4, :],
-                    )
-
-        def load_scales_sw(gate):
-            src = scales[gate].bitcast(F32).rearrange("(hf a) q n -> a hf q n", hf=2)
-            for quad in (0, 2, 1, 3):
-                for r in range(4):
-                    nc.gpsimd.dma_start(
-                        out=planes[32 * quad + r:32 * quad + 16:4, 2 * gate:2 * gate + 2, :].bitcast(F32),
-                        in_=src[:, :, 4 * quad + r, :],
-                    )
+                    for r in range(4):
+                        nc.gpsimd.dma_start(
+                            out=planes[32 * quad + r:32 * quad + 16:4, 2 * gate:2 * gate + 2, :].bitcast(F32),
+                            in_=src[:, :, 4 * quad + r, :],
+                        )
+            else:
+                src = scales[gate].bitcast(I32)
+                for hf in range(2):
+                    for quad in (0, 2, 1, 3):
+                        nc.sync.dma_start(
+                            out=planes[32 * quad:32 * quad + 16, 2 * gate + hf, :].bitcast(I32),
+                            in_=src[4 * hf:4 * hf + 4, 4 * quad:4 * quad + 4, :],
+                        )
 
         def load_rect(gate, g0, g1, c0, c1):
             ng = g1 - g0
@@ -94,7 +87,7 @@ def tile_gru_w_kernel(tc, inp, h, W_r_words, W_r_scales, b_r, W_u_words, W_u_sca
                 for j in range(c0 // P, c1 // P):
                     wmap[(gate, g, j)] = view[:, g - g0, P * j - c0:P * j - c0 + P]
 
-        def mx(ps_ap, gate, g, j):
+        def mx(ps_ap, gate, g, j, start, stop):
             if gate == 2 and g >= 4:
                 rhs = hr_codes[:, g - 4, :]
                 rhs_scale = hr_scales[:, g - 4, :]
@@ -107,19 +100,27 @@ def tile_gru_w_kernel(tc, inp, h, W_r_words, W_r_scales, b_r, W_u_words, W_u_sca
                 lhsT_scale=planes[4 * (g % 4):P, 2 * gate + g // 4, P * j:P * j + P],
                 rhs=rhs.bitcast(FP8X4),
                 rhs_scale=rhs_scale,
-                start=(g == 0),
-                stop=(g == NG - 1),
+                start=start,
+                stop=stop,
             )
 
-        def post(gate, q, ps_list, fine=False):
+        def banks(side):
+            return [psum.tile([P, 4, L], F32, name="acc%s%d" % (side, b), tag="%s%d" % (side, b)) for b in range(4)]
+
+        def passes(acc, gate, g, bank_list):
+            for b in bank_list:
+                for a in range(4):
+                    mx(acc[b][:, a, :], gate, g, 4 * b + a, g == 0 and a == 0, g == NG - 1 and a == 3)
+
+        def post(gate, q, acc_q, fine=False):
             act = work.tile([P, 4, L], F32, name="act", tag="act")
             func = ACT.Tanh if gate == 2 else ACT.Sigmoid
             pieces = [(a, a + 1) for a in range(4)] if fine else [(0, 4)]
-            for a in range(4):
-                col = 16 * gate + 4 * q + a
-                nc.scalar.activation(out=act[:, a, :], in_=ps_list[a], func=func,
-                                     bias=bias[:, col:col + 1], scale=1.0)
             for lo, hi in pieces:
+                for a in range(lo, hi):
+                    col = 16 * gate + 4 * q + a
+                    nc.scalar.activation(out=act[:, a, :], in_=acc_q[:, a, :], func=func,
+                                         bias=bias[:, col:col + 1], scale=1.0)
                 pc = slice(lo, hi)
                 sl = slice(4 * q + lo, 4 * q + hi)
                 if gate == 0:
@@ -135,25 +136,6 @@ def tile_gru_w_kernel(tc, inp, h, W_r_words, W_r_scales, b_r, W_u_words, W_u_sca
                                             op=ALU.add)
                     nc.sync.dma_start(out=out_v[:, sl, :], in_=blend[:, sl, :])
 
-        def live_tiles():
-            return [ps_lv.tile([P, L], F32, name="lv%d" % a, tag="lv%d" % a) for a in range(4)]
-
-        def quad_major(gate, q):
-            jb = ps_jb.tile([P, 4, L], F32, name="jb", tag="jb")
-            for a in range(4):
-                for g in range(NG):
-                    mx(jb[:, a, :], gate, g, 4 * q + a)
-            post(gate, q, [jb[:, a, :] for a in range(4)])
-
-        def gate_by_g(gate):
-            lv = live_tiles()
-            for g in range(NG):
-                for a in range(4):
-                    mx(lv[a][:], gate, g, a)
-            post(gate, 0, [t[:] for t in lv])
-            for q in range(1, 4):
-                quad_major(gate, q)
-
         for gate in range(3):
             nc.vector.memset(planes[:, 2 * gate:2 * gate + 2, :].bitcast(I32), 0)
         nc.vector.memset(b_raw[:], 0.0)
@@ -166,9 +148,8 @@ def tile_gru_w_kernel(tc, inp, h, W_r_words, W_r_scales, b_r, W_u_words, W_u_sca
         for gate in range(3):
             nc.scalar.dma_start(out=b_raw[16 * gate:16 * gate + 16, :],
                                 in_=biases[gate].rearrange("(j m) -> j m", m=P))
-        load_scales_sw(1)
-        load_scales_sw(2)
-        load_scales(0)
+        for gate in range(3):
+            load_scales(gate)
         for gate in range(2):
             for g in range(NG):
                 load_rect(gate, g, g + 1, 0, CH)
@@ -184,12 +165,12 @@ def tile_gru_w_kernel(tc, inp, h, W_r_words, W_r_scales, b_r, W_u_words, W_u_sca
                 in_=x_grp[:, gs, :, :].rearrange("p g l t -> p (g l t)"),
             )
 
-        pb = ps_tp.tile([P, P], BF16, name="pb", tag="tp")
+        pb = psum.tile([P, P], BF16, name="pb", tag="B0")
         nc.tensor.transpose(pb[:], b_raw[:], ident[:])
         nc.vector.tensor_copy(out=bias[:], in_=pb[:])
 
         for b in range(2):
-            pt = ps_tp.tile([P, 8, P], BF16, name="pt", tag="tp")
+            pt = psum.tile([P, 8, P], BF16, name="pt", tag="B%d" % (1 + b))
             for g2 in range(2):
                 for t in range(4):
                     nc.tensor.transpose(pt[:, 4 * g2 + t, :], x_raw[:, 4 + 2 * b + g2, t, :], ident[:])
@@ -200,7 +181,7 @@ def tile_gru_w_kernel(tc, inp, h, W_r_words, W_r_scales, b_r, W_u_words, W_u_sca
             else:
                 nc.scalar.copy(out=dst, in_=src)
         for b in range(2):
-            pc = ps_tp.tile([P, 8, L], BF16, name="pc", tag="tp")
+            pc = psum.tile([P, 8, L], BF16, name="pc", tag="B%d" % (3 * (1 - b)))
             for jj in range(8):
                 nc.tensor.transpose(pc[:, jj, :], hT[:, 1024 * b + P * jj:1024 * b + P * jj + P], ident[:])
             if b == 0:
@@ -208,43 +189,60 @@ def tile_gru_w_kernel(tc, inp, h, W_r_words, W_r_scales, b_r, W_u_words, W_u_sca
             else:
                 nc.scalar.copy(out=h_c[:, 8:16, :], in_=pc[:])
 
-        gate_by_g(0)
+        acc_r = banks("A")
+        for g in range(NG):
+            passes(acc_r, 0, g, range(4))
 
-        for rect in H_RECTS:
-            load_rect(2, rect[0], rect[1], rect[2], rect[3])
-
+        for g in range(6):
+            load_rect(2, g, g + 1, 0, CH)
         for b in range(2):
-            pt = ps_tp.tile([P, 8, P], BF16, name="pt2", tag="tp")
+            load_rect(2, 6, 8, 512 * b, 512 * b + 512)
+
+        def hr_first(b):
+            pt2 = psum.tile([P, 8, P], BF16, name="pt2", tag="A%d" % (2 * b))
             for jj in range(8):
-                nc.tensor.transpose(pt[:, jj, :], hr_c[:, 8 * b + jj, :], ident[:])
+                nc.tensor.transpose(pt2[:, jj, :], hr_c[:, 8 * b + jj, :], ident[:])
             dst = hrT[:, 1024 * b:1024 * b + 1024].rearrange("l (g t p) -> l g t p", g=2, t=4)
-            src = pt[:].rearrange("l j m -> l (j m)").rearrange("l (g p t) -> l g t p", g=2, t=4)
+            src = pt2[:].rearrange("l j m -> l (j m)").rearrange("l (g p t) -> l g t p", g=2, t=4)
             nc.vector.tensor_copy(out=dst, in_=src)
-            pq = ps_tp.tile([P, 8, L], BF16, name="pq", tag="tp")
+
+        def hr_second(b):
+            pq = psum.tile([P, 8, L], BF16, name="pq", tag="A%d" % (2 * b + 1))
             for k in range(8):
                 nc.tensor.transpose(pq[:, k, :], hrT[:, 1024 * b + P * k:1024 * b + P * k + P], ident[:])
             gs = slice(2 * b, 2 * b + 2)
-            nc.scalar.copy(out=hr_grp[:, gs, :, :], in_=pq[:].rearrange("p (g t) l -> p g l t", g=2))
+            nc.vector.tensor_copy(out=hr_grp[:, gs, :, :], in_=pq[:].rearrange("p (g t) l -> p g l t", g=2))
             nc.vector.quantize_mx(
                 out=hr_codes[:, gs, :].rearrange("p g l -> p (g l)").bitcast(FP8X4),
                 scales=hr_scales[:, gs, :].rearrange("p g l -> p (g l)"),
                 in_=hr_grp[:, gs, :, :].rearrange("p g l t -> p (g l t)"),
             )
 
-        gate_by_g(1)
+        acc_u = banks("B")
+        post(0, 0, acc_r[0])
+        post(0, 1, acc_r[1])
+        passes(acc_u, 1, 0, range(4))
+        hr_first(0)
+        post(0, 2, acc_r[2])
+        post(0, 3, acc_r[3])
+        passes(acc_u, 1, 1, range(4))
+        hr_second(0)
+        hr_first(1)
+        passes(acc_u, 1, 2, range(4))
+        hr_second(1)
+        for g in range(3, NG):
+            passes(acc_u, 1, g, range(4))
 
-        lv = live_tiles()
-        for g in range(NG):
-            for a in range(4):
-                mx(lv[a][:], 2, g, a)
-        post(2, 0, [t[:] for t in lv])
-        quad_major(2, 1)
-        lv = live_tiles()
-        for g in range(4):
-            for a in range(4):
-                mx(lv[a][:], 2, g, 12 + a)
-        quad_major(2, 2)
-        for g in range(4, NG):
-            for a in range(4):
-                mx(lv[a][:], 2, g, 12 + a)
-        post(2, 3, [t[:] for t in lv], fine=True)
+        for b in range(2, 4):
+            load_rect(2, 6, 8, 512 * b, 512 * b + 512)
+
+        acc_n = banks("A")
+        passes(acc_n, 2, 0, range(4))
+        for q in range(4):
+            post(1, q, acc_u[q])
+        for g in range(1, 6):
+            passes(acc_n, 2, g, range(4))
+        for b in range(4):
+            passes(acc_n, 2, 6, [b])
+            passes(acc_n, 2, 7, [b])
+            post(2, b, acc_n[b], fine=(b == 3))

@@ -19,7 +19,7 @@ FLOPS = 3 * 2 * 4096 * 2048 * 128
 
 PIN = True
 W_BUFS = 16
-SW_SCALES = (False, True, True)
+SW_SCALES = (False, False, True)
 
 
 def tile_gru_w_kernel(tc, inp, h, W_r_words, W_r_scales, b_r, W_u_words, W_u_scales, b_u,
@@ -148,9 +148,9 @@ def tile_gru_w_kernel(tc, inp, h, W_r_words, W_r_scales, b_r, W_u_words, W_u_sca
         for gate in range(3):
             nc.scalar.dma_start(out=b_raw[16 * gate:16 * gate + 16, :],
                                 in_=biases[gate].rearrange("(j m) -> j m", m=P))
-        for gate in range(3):
-            load_scales(gate)
+        load_scales(2)
         for gate in range(2):
+            load_scales(gate)
             for g in range(NG):
                 load_rect(gate, g, g + 1, 0, CH)
 

@@ -19,7 +19,7 @@ FLOPS = 3 * 2 * 4096 * 2048 * 128
 
 PIN = True
 W_BUFS = 16
-SW_SCALES = (False, False, True)
+SW_SCALES = (True, True, True)
 
 
 def tile_gru_w_kernel(tc, inp, h, W_r_words, W_r_scales, b_r, W_u_words, W_u_scales, b_u,
@@ -61,8 +61,8 @@ def tile_gru_w_kernel(tc, inp, h, W_r_words, W_r_scales, b_r, W_u_words, W_u_sca
         def load_scales(gate):
             if SW_SCALES[gate]:
                 src = scales[gate].bitcast(F32).rearrange("(hf a) q n -> a hf q n", hf=2)
-                for quad in (0, 2, 1, 3):
-                    for r in range(4):
+                for r in range(4):
+                    for quad in (0, 2, 1, 3):
                         nc.gpsimd.dma_start(
                             out=planes[32 * quad + r:32 * quad + 16:4, 2 * gate:2 * gate + 2, :].bitcast(F32),
                             in_=src[:, :, 4 * quad + r, :],
@@ -148,9 +148,9 @@ def tile_gru_w_kernel(tc, inp, h, W_r_words, W_r_scales, b_r, W_u_words, W_u_sca
         for gate in range(3):
             nc.scalar.dma_start(out=b_raw[16 * gate:16 * gate + 16, :],
                                 in_=biases[gate].rearrange("(j m) -> j m", m=P))
-        load_scales(2)
-        for gate in range(2):
+        for gate in range(3):
             load_scales(gate)
+        for gate in range(2):
             for g in range(NG):
                 load_rect(gate, g, g + 1, 0, CH)
 

@@ -193,8 +193,10 @@ def tile_gru_w_kernel(tc, inp, h, W_r_words, W_r_scales, b_r, W_u_words, W_u_sca
         for g in range(NG):
             passes(acc_r, 0, g, range(4))
 
-        for g in range(6):
+        for g in range(4):
             load_rect(2, g, g + 1, 0, CH)
+        for g in range(4, 6):
+            load_rect(2, g, g + 1, 0, 1536)
         for b in range(2):
             load_rect(2, 6, 8, 512 * b, 512 * b + 512)
 
@@ -233,16 +235,53 @@ def tile_gru_w_kernel(tc, inp, h, W_r_words, W_r_scales, b_r, W_u_words, W_u_sca
         for g in range(3, NG):
             passes(acc_u, 1, g, range(4))
 
-        for b in range(2, 4):
-            load_rect(2, 6, 8, 512 * b, 512 * b + 512)
+        load_rect(2, 6, 8, 1024, 1536)
+        load_rect(2, 4, 6, 1536, 2048)
+        load_rect(2, 6, 8, 1536, 1792)
+        load_rect(2, 6, 8, 1792, 1920)
+        load_rect(2, 6, 8, 1920, 2048)
 
-        acc_n = banks("A")
-        passes(acc_n, 2, 0, range(4))
+        def n_group(tag, blocks):
+            return (psum.tile([P, 4, L], F32, name="accn" + tag, tag=tag), blocks)
+
+        def n_passes(g, groups):
+            for acc, blocks in groups:
+                for i, j in enumerate(blocks):
+                    mx(acc[:, i, :], 2, g, j, g == 0 and i == 0, g == NG - 1 and i == len(blocks) - 1)
+
+        def n_post(group):
+            acc, blocks = group
+            n = len(blocks)
+            act = work.tile([P, 4, L], F32, name="act", tag="act")
+            for i, j in enumerate(blocks):
+                nc.scalar.activation(out=act[:, i, :], in_=acc[:, i, :], func=ACT.Tanh,
+                                     bias=bias[:, 32 + j:33 + j], scale=1.0)
+            sl = slice(blocks[0], blocks[0] + n)
+            nc.vector.tensor_tensor(out=act[:, 0:n, :], in0=act[:, 0:n, :], in1=one_minus_u[:, sl, :], op=ALU.mult)
+            nc.vector.tensor_tensor(out=blend[:, sl, :], in0=act[:, 0:n, :], in1=blend[:, sl, :], op=ALU.add)
+            nc.sync.dma_start(out=out_v[:, sl, :], in_=blend[:, sl, :])
+
+        early = [n_group("A%d" % b, [4 * b + a for a in range(4)]) for b in range(3)]
+        late = [n_group("A3", [12, 13])]
+        n_passes(0, early + late)
         for q in range(4):
             post(1, q, acc_u[q])
-        for g in range(1, 6):
-            passes(acc_n, 2, g, range(4))
-        for b in range(4):
-            passes(acc_n, 2, 6, [b])
-            passes(acc_n, 2, 7, [b])
-            post(2, b, acc_n[b], fine=(b == 3))
+        n_passes(1, early + late)
+        last = [n_group("B0", [14]), n_group("B1", [15])]
+        n_passes(0, last)
+        n_passes(1, last)
+        late = late + last
+        for g in range(2, 4):
+            n_passes(g, early + late)
+        for g in range(4, 6):
+            n_passes(g, early)
+        for group in early:
+            n_passes(6, [group])
+            n_passes(7, [group])
+            n_post(group)
+        for g in range(4, 6):
+            n_passes(g, late)
+        for group in late:
+            n_passes(6, [group])
+            n_passes(7, [group])
+            n_post(group)

@@ -62,7 +62,7 @@ def tile_gru_w_kernel(tc, inp, h, W_r_words, W_r_scales, b_r, W_u_words, W_u_sca
             if SW_SCALES[gate]:
                 src = scales[gate].bitcast(F32).rearrange("(hf a) q n -> a hf q n", hf=2)
                 for r in range(4):
-                    for quad in (0, 2, 1, 3):
+                    for quad in (0, 1, 2, 3):
                         nc.gpsimd.dma_start(
                             out=planes[32 * quad + r:32 * quad + 16:4, 2 * gate:2 * gate + 2, :].bitcast(F32),
                             in_=src[:, :, 4 * quad + r, :],

@@ -156,7 +156,7 @@ def tile_gru_w_kernel(tc, inp, h, W_r_words, W_r_scales, b_r, W_u_words, W_u_sca
 
         for half in (1, 0):
             gs = slice(4 * half, 4 * half + 4)
-            nc.vector.tensor_copy(out=x_grp[:, gs, :, :], in_=x_raw[:, gs, :, :].rearrange("p g t l -> p g l t"))
+            nc.scalar.copy(out=x_grp[:, gs, :, :], in_=x_raw[:, gs, :, :].rearrange("p g t l -> p g l t"))
         for half in (1, 0):
             gs = slice(4 * half, 4 * half + 4)
             nc.vector.quantize_mx(

@@ -19,7 +19,6 @@ FLOPS = 3 * 2 * 4096 * 2048 * 128
 
 PIN = True
 W_BUFS = 16
-SW_SCALES = (True, True, True)
 
 
 def tile_gru_w_kernel(tc, inp, h, W_r_words, W_r_scales, b_r, W_u_words, W_u_scales, b_u,
@@ -56,25 +55,30 @@ def tile_gru_w_kernel(tc, inp, h, W_r_words, W_r_scales, b_r, W_u_words, W_u_sca
         one_minus_u = const.tile([P, 16, L], F32, name="one_minus_u")
         blend = const.tile([P, 16, L], F32, name="blend")
 
+        spare = const.tile([P, 24, 2, 48], BF16, name="spare")
+
         wmap = {}
 
+        fillers = []
+
+        def step_cursor(q0):
+            i = len(fillers)
+            fillers.append(i)
+            nc.gpsimd.dma_start(
+                out=spare[q0 + 16:q0 + 32:4, i, :, 0:32],
+                in_=b_h.rearrange("(a b c) -> a b c", a=4, b=2)[:, :, 32 * (i % 8):32 * (i % 8) + 32],
+            )
+
         def load_scales(gate):
-            if SW_SCALES[gate]:
-                src = scales[gate].bitcast(F32).rearrange("(hf a) q n -> a hf q n", hf=2)
-                for r in range(4):
-                    for quad in (0, 1, 2, 3):
-                        nc.gpsimd.dma_start(
-                            out=planes[32 * quad + r:32 * quad + 16:4, 2 * gate:2 * gate + 2, :].bitcast(F32),
-                            in_=src[:, :, 4 * quad + r, :],
-                        )
-            else:
-                src = scales[gate].bitcast(I32)
+            src = scales[gate].bitcast(F32)
+            for pair in range(2):
                 for hf in range(2):
-                    for quad in (0, 2, 1, 3):
-                        nc.sync.dma_start(
-                            out=planes[32 * quad:32 * quad + 16, 2 * gate + hf, :].bitcast(I32),
+                    for quad in (pair, pair + 2):
+                        nc.gpsimd.dma_start(
+                            out=planes[32 * quad:32 * quad + 16, 2 * gate + hf, :].bitcast(F32),
                             in_=src[4 * hf:4 * hf + 4, 4 * quad:4 * quad + 4, :],
                         )
+                        step_cursor(64 * (quad // 2))
 
         def load_rect(gate, g0, g1, c0, c1):
             ng = g1 - g0

@@ -71,14 +71,17 @@ def tile_gru_w_kernel(tc, inp, h, W_r_words, W_r_scales, b_r, W_u_words, W_u_sca
 
         def load_scales(gate):
             src = scales[gate].bitcast(F32)
-            for pair in range(2):
-                for hf in range(2):
-                    for quad in (pair, pair + 2):
-                        nc.gpsimd.dma_start(
-                            out=planes[32 * quad:32 * quad + 16, 2 * gate + hf, :].bitcast(F32),
-                            in_=src[4 * hf:4 * hf + 4, 4 * quad:4 * quad + 4, :],
-                        )
-                        step_cursor(64 * (quad // 2))
+            for quad in (0, 2, 1, 3):
+                nc.gpsimd.dma_start(
+                    out=planes[32 * quad:32 * quad + 32, 2 * gate, :].bitcast(F32),
+                    in_=src[:, 4 * quad:4 * quad + 4, :],
+                )
+            for quad in (0, 2, 1, 3):
+                nc.gpsimd.dma_start(
+                    out=planes[32 * quad:32 * quad + 16, 2 * gate + 1, :].bitcast(F32),
+                    in_=src[4:8, 4 * quad:4 * quad + 4, :],
+                )
+                step_cursor(64 * (quad // 2))
 
         def load_rect(gate, g0, g1, c0, c1):
             ng = g1 - g0

@@ -37,25 +37,25 @@ def tile_gru_w_kernel(tc, inp, h, W_r_words, W_r_scales, b_r, W_u_words, W_u_sca
         if PIN:
             ctx.enter_context(tc.manual_schedule())
 
-        planes = const.tile([P, 6, CH], U8, name="planes", align_bytes=64)
-        x_raw = const.tile([P, NG, 4, L], BF16, name="x_raw")
-        x_grp = const.tile([P, NG, L, 4], BF16, name="x_grp", align_bytes=64)
-        x_codes = const.tile([P, NG, L], I32, name="x_codes", align_bytes=64)
-        x_scales = const.tile([P, NG, L], U8, name="x_scales", align_bytes=64)
+        planes = const.tile([P, 6, CH], U8, name="planes", align_bytes=256)
+        x_raw = const.tile([P, NG, 4, L], BF16, name="x_raw", align_bytes=256)
+        x_grp = const.tile([P, NG, L, 4], BF16, name="x_grp", align_bytes=256)
+        x_codes = const.tile([P, NG, L], I32, name="x_codes", align_bytes=256)
+        x_scales = const.tile([P, NG, L], U8, name="x_scales", align_bytes=256)
         ident = const.tile([P, P], BF16, name="ident")
-        b_raw = const.tile([P, P], BF16, name="b_raw")
+        b_raw = const.tile([P, P], BF16, name="b_raw", align_bytes=256)
         bias = const.tile([P, P], F32, name="bias")
         hT = const.tile([P, CH], BF16, name="hT")
         h_c = const.tile([P, 16, L], BF16, name="h_c")
         hr_c = const.tile([P, 16, L], BF16, name="hr_c")
         hrT = const.tile([P, CH], BF16, name="hrT")
-        hr_grp = const.tile([P, 4, L, 4], BF16, name="hr_grp", align_bytes=64)
-        hr_codes = const.tile([P, 4, L], I32, name="hr_codes", align_bytes=64)
-        hr_scales = const.tile([P, 4, L], U8, name="hr_scales", align_bytes=64)
-        one_minus_u = const.tile([P, 16, L], F32, name="one_minus_u")
-        blend = const.tile([P, 16, L], F32, name="blend")
+        hr_grp = const.tile([P, 4, L, 4], BF16, name="hr_grp", align_bytes=256)
+        hr_codes = const.tile([P, 4, L], I32, name="hr_codes", align_bytes=256)
+        hr_scales = const.tile([P, 4, L], U8, name="hr_scales", align_bytes=256)
+        one_minus_u = const.tile([P, 16, L], F32, name="one_minus_u", align_bytes=256)
+        blend = const.tile([P, 16, L], F32, name="blend", align_bytes=256)
 
-        spare = const.tile([P, 24, 2, 48], BF16, name="spare")
+        spare = const.tile([P, 24, 2, 48], BF16, name="spare", align_bytes=256)
 
         wmap = {}
 
@@ -86,7 +86,7 @@ def tile_gru_w_kernel(tc, inp, h, W_r_words, W_r_scales, b_r, W_u_words, W_u_sca
         def load_rect(gate, g0, g1, c0, c1):
             ng = g1 - g0
             ncol = c1 - c0
-            wt = wpool.tile([P, CH], I32, name="wt", tag="w", align_bytes=64)
+            wt = wpool.tile([P, CH], I32, name="wt", tag="w", align_bytes=256)
             view = wt[:, 0:ng * ncol].rearrange("p (g n) -> p g n", g=ng)
             src = words[gate].rearrange("g p n t -> p g (n t)")[:, g0:g1, 4 * c0:4 * c1].bitcast(I32)
             nc.sync.dma_start(out=view, in_=src)

@@ -245,8 +245,7 @@ def tile_gru_w_kernel(tc, inp, h, W_r_words, W_r_scales, b_r, W_u_words, W_u_sca
         load_rect(2, 6, 8, 1024, 1536)
         load_rect(2, 4, 6, 1536, 2048)
         load_rect(2, 6, 8, 1536, 1792)
-        load_rect(2, 6, 8, 1792, 1920)
-        load_rect(2, 6, 8, 1920, 2048)
+        load_rect(2, 6, 8, 1792, 2048)
 
         def n_group(tag, blocks):
             return (psum.tile([P, 4, L], F32, name="accn" + tag, tag=tag), blocks)
@@ -264,8 +263,13 @@ def tile_gru_w_kernel(tc, inp, h, W_r_words, W_r_scales, b_r, W_u_words, W_u_sca
                 nc.scalar.activation(out=act[:, i, :], in_=acc[:, i, :], func=ACT.Tanh,
                                      bias=bias[:, 32 + j:33 + j], scale=1.0)
             sl = slice(blocks[0], blocks[0] + n)
-            nc.vector.tensor_tensor(out=act[:, 0:n, :], in0=act[:, 0:n, :], in1=one_minus_u[:, sl, :], op=ALU.mult)
-            nc.vector.tensor_tensor(out=blend[:, sl, :], in0=act[:, 0:n, :], in1=blend[:, sl, :], op=ALU.add)
+            halves = (slice(0, n // 2), slice(n // 2, n))
+            for hs in halves:
+                nc.vector.tensor_tensor(out=act[:, hs, :], in0=act[:, hs, :],
+                                        in1=one_minus_u[:, sl, :][:, hs, :], op=ALU.mult)
+            for hs in halves:
+                nc.vector.tensor_tensor(out=blend[:, sl, :][:, hs, :], in0=act[:, hs, :],
+                                        in1=blend[:, sl, :][:, hs, :], op=ALU.add)
             nc.sync.dma_start(out=out_v[:, sl, :], in_=blend[:, sl, :])
 
         early = [n_group("A%d" % b, [4 * b + a for a in range(4)]) for b in range(3)]
@@ -274,7 +278,7 @@ def tile_gru_w_kernel(tc, inp, h, W_r_words, W_r_scales, b_r, W_u_words, W_u_sca
         for q in range(4):
             post(1, q, acc_u[q])
         n_passes(1, early + late)
-        last = [n_group("B0", [14]), n_group("B1", [15])]
+        last = [n_group("B0", [14, 15])]
         n_passes(0, last)
         n_passes(1, last)
         late = late + last

@@ -18,7 +18,7 @@ NG = 8
 FLOPS = 3 * 2 * 4096 * 2048 * 128
 
 PIN = True
-W_BUFS = 16
+W_BUFS = 8
 
 
 def tile_gru_w_kernel(tc, inp, h, W_r_words, W_r_scales, b_r, W_u_words, W_u_scales, b_u,
@@ -83,11 +83,13 @@ def tile_gru_w_kernel(tc, inp, h, W_r_words, W_r_scales, b_r, W_u_words, W_u_sca
                 )
                 step_cursor(64 * (quad // 2))
 
-        def load_rect(gate, g0, g1, c0, c1):
+        def word_tile():
+            return wpool.tile([P, 2 * CH], I32, name="wt", tag="w", align_bytes=256)
+
+        def load_rect(wt, at, gate, g0, g1, c0, c1):
             ng = g1 - g0
             ncol = c1 - c0
-            wt = wpool.tile([P, CH], I32, name="wt", tag="w", align_bytes=256)
-            view = wt[:, 0:ng * ncol].rearrange("p (g n) -> p g n", g=ng)
+            view = wt[:, at:at + ng * ncol].rearrange("p (g n) -> p g n", g=ng)
             src = words[gate].rearrange("g p n t -> p g (n t)")[:, g0:g1, 4 * c0:4 * c1].bitcast(I32)
             nc.sync.dma_start(out=view, in_=src)
             for g in range(g0, g1):
@@ -158,8 +160,8 @@ def tile_gru_w_kernel(tc, inp, h, W_r_words, W_r_scales, b_r, W_u_words, W_u_sca
         for gate in range(3):
             load_scales(gate)
         for gate in range(2):
-            for g in range(NG):
-                load_rect(gate, g, g + 1, 0, CH)
+            for g in range(0, NG, 2):
+                load_rect(word_tile(), 0, gate, g, g + 2, 0, CH)
 
         for half in (1, 0):
             gs = slice(4 * half, 4 * half + 4)
@@ -200,12 +202,14 @@ def tile_gru_w_kernel(tc, inp, h, W_r_words, W_r_scales, b_r, W_u_words, W_u_sca
         for g in range(NG):
             passes(acc_r, 0, g, range(4))
 
-        for g in range(4):
-            load_rect(2, g, g + 1, 0, CH)
+        for g in (0, 2):
+            load_rect(word_tile(), 0, 2, g, g + 2, 0, CH)
+        wt_45 = word_tile()
         for g in range(4, 6):
-            load_rect(2, g, g + 1, 0, 1536)
-        for b in range(2):
-            load_rect(2, 6, 8, 512 * b, 512 * b + 512)
+            load_rect(wt_45, 1536 * (g - 4), 2, g, g + 1, 0, 1536)
+        wt_67 = word_tile()
+        for b in range(3):
+            load_rect(wt_67, 1024 * b, 2, 6, 8, 512 * b, 512 * b + 512)
 
         def hr_first(b):
             pt2 = psum.tile([P, 8, P], BF16, name="pt2", tag="A%d" % (2 * b))
@@ -242,10 +246,10 @@ def tile_gru_w_kernel(tc, inp, h, W_r_words, W_r_scales, b_r, W_u_words, W_u_sca
         for g in range(3, NG):
             passes(acc_u, 1, g, range(4))
 
-        load_rect(2, 6, 8, 1024, 1536)
-        load_rect(2, 4, 6, 1536, 2048)
-        load_rect(2, 6, 8, 1536, 1792)
-        load_rect(2, 6, 8, 1792, 2048)
+        wt_last = word_tile()
+        load_rect(wt_last, 0, 2, 4, 6, 1536, 2048)
+        load_rect(wt_last, 1024, 2, 6, 8, 1536, 1792)
+        load_rect(wt_last, 1536, 2, 6, 8, 1792, 2048)
 
         def n_group(tag, blocks):
             return (psum.tile([P, 4, L], F32, name="accn" + tag, tag=tag), blocks)

from contextlib import ExitStack

import concourse.mybir as mybir
from concourse.masks import make_identity

FP8X4 = mybir.dt.float8_e4m3fn_x4
BF16 = mybir.dt.bfloat16
F32 = mybir.dt.float32
I32 = mybir.dt.int32
U8 = mybir.dt.uint8
ACT = mybir.ActivationFunctionType
ALU = mybir.AluOpType

P = 128
L = 128
CH = 2048
NG = 8
FLOPS = 3 * 2 * 4096 * 2048 * 128

PIN = True
W_BUFS = 8


def tile_gru_w_kernel(tc, inp, h, W_r_words, W_r_scales, b_r, W_u_words, W_u_scales, b_u,
                                 W_h_words, W_h_scales, b_h, out):
    nc = tc.nc
    words = (W_r_words, W_u_words, W_h_words)
    scales = (W_r_scales, W_u_scales, W_h_scales)
    biases = (b_r, b_u, b_h)
    out_v = out[0].rearrange("(j m) l -> m j l", m=P)

    with ExitStack() as ctx:
        const = ctx.enter_context(tc.tile_pool(name="const", bufs=1))
        wpool = ctx.enter_context(tc.tile_pool(name="wpool", bufs=W_BUFS))
        work = ctx.enter_context(tc.tile_pool(name="work", bufs=4))
        psum = ctx.enter_context(tc.psum_pool(name="psum", bufs=1))
        if PIN:
            ctx.enter_context(tc.manual_schedule())

        planes = const.tile([P, 6, CH], U8, name="planes", align_bytes=256)
        x_raw = const.tile([P, NG, 4, L], BF16, name="x_raw", align_bytes=256)
        x_grp = const.tile([P, NG, L, 4], BF16, name="x_grp", align_bytes=256)
        x_codes = const.tile([P, NG, L], I32, name="x_codes", align_bytes=256)
        x_scales = const.tile([P, NG, L], U8, name="x_scales", align_bytes=256)
        ident = const.tile([P, P], BF16, name="ident")
        b_raw = const.tile([P, P], BF16, name="b_raw", align_bytes=256)
        bias = const.tile([P, P], F32, name="bias")
        hT = const.tile([P, CH], BF16, name="hT")
        h_c = const.tile([P, 16, L], BF16, name="h_c")
        hr_c = const.tile([P, 16, L], BF16, name="hr_c")
        hrT = const.tile([P, CH], BF16, name="hrT")
        hr_grp = const.tile([P, 4, L, 4], BF16, name="hr_grp", align_bytes=256)
        hr_codes = const.tile([P, 4, L], I32, name="hr_codes", align_bytes=256)
        hr_scales = const.tile([P, 4, L], U8, name="hr_scales", align_bytes=256)
        one_minus_u = const.tile([P, 16, L], F32, name="one_minus_u", align_bytes=256)
        blend = const.tile([P, 16, L], F32, name="blend", align_bytes=256)

        spare = const.tile([P, 24, 2, 48], BF16, name="spare", align_bytes=256)

        wmap = {}

        fillers = []

        def step_cursor(q0):
            i = len(fillers)
            fillers.append(i)
            nc.gpsimd.dma_start(
                out=spare[q0 + 16:q0 + 32:4, i, :, 0:32],
                in_=b_h.rearrange("(a b c) -> a b c", a=4, b=2)[:, :, 32 * (i % 8):32 * (i % 8) + 32],
            )

        def load_scales(gate):
            src = scales[gate].bitcast(F32)
            for quad in (0, 2, 1, 3):
                nc.gpsimd.dma_start(
                    out=planes[32 * quad:32 * quad + 32, 2 * gate, :].bitcast(F32),
                    in_=src[:, 4 * quad:4 * quad + 4, :],
                )
            for quad in (0, 2, 1, 3):
                nc.gpsimd.dma_start(
                    out=planes[32 * quad:32 * quad + 16, 2 * gate + 1, :].bitcast(F32),
                    in_=src[4:8, 4 * quad:4 * quad + 4, :],
                )
                step_cursor(64 * (quad // 2))

        def word_tile():
            return wpool.tile([P, 2 * CH], I32, name="wt", tag="w", align_bytes=256)

        def load_rect(wt, at, gate, g0, g1, c0, c1):
            ng = g1 - g0
            ncol = c1 - c0
            view = wt[:, at:at + ng * ncol].rearrange("p (g n) -> p g n", g=ng)
            src = words[gate].rearrange("g p n t -> p g (n t)")[:, g0:g1, 4 * c0:4 * c1].bitcast(I32)
            nc.sync.dma_start(out=view, in_=src)
            for g in range(g0, g1):
                for j in range(c0 // P, c1 // P):
                    wmap[(gate, g, j)] = view[:, g - g0, P * j - c0:P * j - c0 + P]

        def mx(ps_ap, gate, g, j, start, stop):
            if gate == 2 and g >= 4:
                rhs = hr_codes[:, g - 4, :]
                rhs_scale = hr_scales[:, g - 4, :]
            else:
                rhs = x_codes[:, g, :]
                rhs_scale = x_scales[:, g, :]
            nc.tensor.matmul_mx(
                out=ps_ap,
                lhsT=wmap[(gate, g, j)].bitcast(FP8X4),
                lhsT_scale=planes[4 * (g % 4):P, 2 * gate + g // 4, P * j:P * j + P],
                rhs=rhs.bitcast(FP8X4),
                rhs_scale=rhs_scale,
                start=start,
                stop=stop,
            )

        def banks(side):
            return [psum.tile([P, 4, L], F32, name="acc%s%d" % (side, b), tag="%s%d" % (side, b)) for b in range(4)]

        def passes(acc, gate, g, bank_list):
            for b in bank_list:
                for a in range(4):
                    mx(acc[b][:, a, :], gate, g, 4 * b + a, g == 0 and a == 0, g == NG - 1 and a == 3)

        def post(gate, q, acc_q, fine=False):
            act = work.tile([P, 4, L], F32, name="act", tag="act")
            func = ACT.Tanh if gate == 2 else ACT.Sigmoid
            pieces = [(a, a + 1) for a in range(4)] if fine else [(0, 4)]
            for lo, hi in pieces:
                for a in range(lo, hi):
                    col = 16 * gate + 4 * q + a
                    nc.scalar.activation(out=act[:, a, :], in_=acc_q[:, a, :], func=func,
                                         bias=bias[:, col:col + 1], scale=1.0)
                pc = slice(lo, hi)
                sl = slice(4 * q + lo, 4 * q + hi)
                if gate == 0:
                    nc.vector.tensor_tensor(out=hr_c[:, sl, :], in0=act[:, pc, :], in1=h_c[:, sl, :], op=ALU.mult)
                elif gate == 1:
                    nc.vector.tensor_scalar(out=one_minus_u[:, sl, :], in0=act[:, pc, :], scalar1=-1.0,
                                            scalar2=1.0, op0=ALU.mult, op1=ALU.add)
                    nc.vector.tensor_tensor(out=blend[:, sl, :], in0=act[:, pc, :], in1=h_c[:, sl, :], op=ALU.mult)
                else:
                    nc.vector.tensor_tensor(out=act[:, pc, :], in0=act[:, pc, :], in1=one_minus_u[:, sl, :],
                                            op=ALU.mult)
                    nc.vector.tensor_tensor(out=blend[:, sl, :], in0=act[:, pc, :], in1=blend[:, sl, :],
                                            op=ALU.add)
                    nc.sync.dma_start(out=out_v[:, sl, :], in_=blend[:, sl, :])

        for gate in range(3):
            nc.vector.memset(planes[:, 2 * gate:2 * gate + 2, :].bitcast(I32), 0)
        nc.vector.memset(b_raw[:], 0.0)
        make_identity(nc, ident[:])

        nc.sync.dma_start(out=x_raw[:, 4:8, :, :].rearrange("p g t l -> p g (t l)"),
                          in_=h[0].rearrange("(g p t) l -> p g (t l)", g=4, p=P, t=4))
        nc.sync.dma_start(out=x_raw[:, 0:4, :, :].rearrange("p g t l -> p g (t l)"),
                          in_=inp[0].rearrange("(g p t) l -> p g (t l)", g=4, p=P, t=4))
        for gate in range(3):
            nc.scalar.dma_start(out=b_raw[16 * gate:16 * gate + 16, :],
                                in_=biases[gate].rearrange("(j m) -> j m", m=P))
        for gate in range(3):
            load_scales(gate)
        for gate in range(2):
            for g in range(0, NG, 2):
                load_rect(word_tile(), 0, gate, g, g + 2, 0, CH)

        for half in (1, 0):
            gs = slice(4 * half, 4 * half + 4)
            nc.scalar.copy(out=x_grp[:, gs, :, :], in_=x_raw[:, gs, :, :].rearrange("p g t l -> p g l t"))
        for half in (1, 0):
            gs = slice(4 * half, 4 * half + 4)
            nc.vector.quantize_mx(
                out=x_codes[:, gs, :].rearrange("p g l -> p (g l)").bitcast(FP8X4),
                scales=x_scales[:, gs, :].rearrange("p g l -> p (g l)"),
                in_=x_grp[:, gs, :, :].rearrange("p g l t -> p (g l t)"),
            )

        pb = psum.tile([P, P], BF16, name="pb", tag="B0")
        nc.tensor.transpose(pb[:], b_raw[:], ident[:])
        nc.vector.tensor_copy(out=bias[:], in_=pb[:])

        for b in range(2):
            pt = psum.tile([P, 8, P], BF16, name="pt", tag="B%d" % (1 + b))
            for g2 in range(2):
                for t in range(4):
                    nc.tensor.transpose(pt[:, 4 * g2 + t, :], x_raw[:, 4 + 2 * b + g2, t, :], ident[:])
            dst = hT[:, 1024 * b:1024 * b + 1024].rearrange("l (g p t) -> l g p t", g=2, t=4)
            src = pt[:].rearrange("l (g t) p -> l g p t", g=2)
            if b == 0:
                nc.vector.tensor_copy(out=dst, in_=src)
            else:
                nc.scalar.copy(out=dst, in_=src)
        for b in range(2):
            pc = psum.tile([P, 8, L], BF16, name="pc", tag="B%d" % (3 * (1 - b)))
            for jj in range(8):
                nc.tensor.transpose(pc[:, jj, :], hT[:, 1024 * b + P * jj:1024 * b + P * jj + P], ident[:])
            if b == 0:
                nc.vector.tensor_copy(out=h_c[:, 0:8, :], in_=pc[:])
            else:
                nc.scalar.copy(out=h_c[:, 8:16, :], in_=pc[:])

        acc_r = banks("A")
        for g in range(NG):
            passes(acc_r, 0, g, range(4))

        for g in (0, 2):
            load_rect(word_tile(), 0, 2, g, g + 2, 0, CH)
        wt_45 = word_tile()
        for g in range(4, 6):
            load_rect(wt_45, 1536 * (g - 4), 2, g, g + 1, 0, 1536)
        wt_67 = word_tile()
        for b in range(3):
            load_rect(wt_67, 1024 * b, 2, 6, 8, 512 * b, 512 * b + 512)

        def hr_first(b):
            pt2 = psum.tile([P, 8, P], BF16, name="pt2", tag="A%d" % (2 * b))
            for jj in range(8):
                nc.tensor.transpose(pt2[:, jj, :], hr_c[:, 8 * b + jj, :], ident[:])
            dst = hrT[:, 1024 * b:1024 * b + 1024].rearrange("l (g t p) -> l g t p", g=2, t=4)
            src = pt2[:].rearrange("l j m -> l (j m)").rearrange("l (g p t) -> l g t p", g=2, t=4)
            nc.vector.tensor_copy(out=dst, in_=src)

        def hr_second(b):
            pq = psum.tile([P, 8, L], BF16, name="pq", tag="A%d" % (2 * b + 1))
            for k in range(8):
                nc.tensor.transpose(pq[:, k, :], hrT[:, 1024 * b + P * k:1024 * b + P * k + P], ident[:])
            gs = slice(2 * b, 2 * b + 2)
            nc.vector.tensor_copy(out=hr_grp[:, gs, :, :], in_=pq[:].rearrange("p (g t) l -> p g l t", g=2))
            nc.vector.quantize_mx(
                out=hr_codes[:, gs, :].rearrange("p g l -> p (g l)").bitcast(FP8X4),
                scales=hr_scales[:, gs, :].rearrange("p g l -> p (g l)"),
                in_=hr_grp[:, gs, :, :].rearrange("p g l t -> p (g l t)"),
            )

        acc_u = banks("B")
        post(0, 0, acc_r[0])
        post(0, 1, acc_r[1])
        passes(acc_u, 1, 0, range(4))
        hr_first(0)
        post(0, 2, acc_r[2])
        post(0, 3, acc_r[3])
        passes(acc_u, 1, 1, range(4))
        hr_second(0)
        hr_first(1)
        passes(acc_u, 1, 2, range(4))
        hr_second(1)
        for g in range(3, NG):
            passes(acc_u, 1, g, range(4))

        wt_last = word_tile()
        load_rect(wt_last, 0, 2, 4, 6, 1536, 2048)
        load_rect(wt_last, 1024, 2, 6, 8, 1536, 1792)
        load_rect(wt_last, 1536, 2, 6, 8, 1792, 2048)

        def n_group(tag, blocks):
            return (psum.tile([P, 4, L], F32, name="accn" + tag, tag=tag), blocks)

        def n_passes(g, groups):
            for acc, blocks in groups:
                for i, j in enumerate(blocks):
                    mx(acc[:, i, :], 2, g, j, g == 0 and i == 0, g == NG - 1 and i == len(blocks) - 1)

        def n_post(group):
            acc, blocks = group
            n = len(blocks)
            act = work.tile([P, 4, L], F32, name="act", tag="act")
            for i, j in enumerate(blocks):
                nc.scalar.activation(out=act[:, i, :], in_=acc[:, i, :], func=ACT.Tanh,
                                     bias=bias[:, 32 + j:33 + j], scale=1.0)
            sl = slice(blocks[0], blocks[0] + n)
            halves = (slice(0, n // 2), slice(n // 2, n))
            for hs in halves:
                nc.vector.tensor_tensor(out=act[:, hs, :], in0=act[:, hs, :],
                                        in1=one_minus_u[:, sl, :][:, hs, :], op=ALU.mult)
            for hs in halves:
                nc.vector.tensor_tensor(out=blend[:, sl, :][:, hs, :], in0=act[:, hs, :],
                                        in1=blend[:, sl, :][:, hs, :], op=ALU.add)
            nc.sync.dma_start(out=out_v[:, sl, :], in_=blend[:, sl, :])

        early = [n_group("A%d" % b, [4 * b + a for a in range(4)]) for b in range(3)]
        late = [n_group("A3", [12, 13])]
        n_passes(0, early + late)
        for q in range(4):
            post(1, q, acc_u[q])
        n_passes(1, early + late)
        last = [n_group("B0", [14, 15])]
        n_passes(0, last)
        n_passes(1, last)
        late = late + last
        for g in range(2, 4):
            n_passes(g, early + late)
        for g in range(4, 6):
            n_passes(g, early)
        for group in early:
            n_passes(6, [group])
            n_passes(7, [group])
            n_post(group)
        for g in range(4, 6):
            n_passes(g, late)
        for group in late:
            n_passes(6, [group])
            n_passes(7, [group])
            n_post(group)
